import numpy as np
import ml_dtypes


def mxq(x, axis, fmt="e4m3"):
    dtype, down = {"e4m3": (ml_dtypes.float8_e4m3fn, 7), "e5m2": (ml_dtypes.float8_e5m2, 14)}[fmt]
    v = np.moveaxis(np.asarray(x, np.float32).astype(ml_dtypes.bfloat16).astype(np.float64), axis, -1)
    blocks = v.reshape(v.shape[:-1] + (-1, 32))
    amax = np.abs(blocks).max(-1, keepdims=True)
    byte = np.maximum(np.where(amax > 0, np.frexp(amax)[1] - 1 + 127, 0) - down, 1)
    scale = np.exp2(byte - 127.0)
    codes = (blocks / scale).astype(np.float32).astype(dtype).astype(np.float64)
    return np.moveaxis((codes * scale).reshape(v.shape), -1, axis)


WIDE = False


def mx_kscale(k):
    if not WIDE:
        return np.ones(k)
    levels = np.array([10, -10, 5, -5, 0])
    if k % 512:
        return np.exp2(np.random.permutation(np.resize(levels, k // 32))).repeat(32)
    a = np.empty((k // 512, 16))
    for p in range(k // 512):
        a[p, :8] = np.random.permutation(np.resize(levels, 8))
        for g in range(8):
            far = levels[np.abs(levels - a[p, g]) >= 10]
            a[p, g + 8] = far[np.random.randint(len(far))]
    return np.exp2(a.ravel()).repeat(32)


BF16 = ml_dtypes.bfloat16


def bf(x):
    return np.asarray(x, np.float32).astype(BF16)


def f64(x):
    return np.asarray(x).astype(np.float64)


N_A, N_P, D = 512, 512, 8192
TEMPERATURE = 0.07
SIG = 3.5
SA = np.sqrt(SIG * TEMPERATURE / np.sqrt(D))
SP = SA * np.sqrt(SIG ** 2 - 2.0 * np.log(N_P / N_A)) / SIG


def logsumexp(v):
    m = v.max(axis=1, keepdims=True)
    return m[:, 0] + np.log(np.exp(v - m).sum(axis=1))


def setup_inputs():
    s = mx_kscale(D)
    c = np.mean(s ** 4) ** -0.25
    return {"anchor": bf(np.random.standard_normal((N_A, D)) * SA * s * c),
            "pos": bf(np.random.standard_normal((N_P, D)) * SP / (s * c))}


def reference(anchor, pos):
    aq = mxq(f64(anchor), 1, "e4m3")
    sim_pos = (aq @ mxq(f64(pos), 1, "e4m3").T) / TEMPERATURE
    sim_neg = (aq @ aq.T) / TEMPERATURE
    sim_neg = np.where(np.eye(aq.shape[0], dtype=bool), -np.inf, sim_neg)
    numerator = logsumexp(sim_pos)
    denominator = np.logaddexp(numerator, logsumexp(sim_neg))
    return numerator - denominator

@@ -1,0 +1,261 @@
+from contextlib import ExitStack
+
+import concourse.masks as masks
+import concourse.mybir as mybir
+
+F32 = mybir.dt.float32
+BF16 = mybir.dt.bfloat16
+U32 = mybir.dt.uint32
+U8 = mybir.dt.uint8
+FP8X4 = mybir.dt.float8_e4m3fn_x4
+ACT = mybir.ActivationFunctionType
+ALU = mybir.AluOpType
+
+P = 128
+PACK = 4
+K_PASS = P * PACK
+BLOCKS = K_PASS // 32
+ROWS = 512
+ROW_TILES = ROWS // P
+HALF = ROWS // 2
+HALF_TILES = HALF // P
+FEATURES = 8192
+PASSES = FEATURES // K_PASS
+LOAD_PASSES = 4
+LOAD_FEATURES = LOAD_PASSES * K_PASS
+LOADS = FEATURES // LOAD_FEATURES
+ALL_LOADS = 4 * LOADS
+LOADS_AHEAD = 6
+TEMPERATURE = 0.07
+MASKED = -1.0e30
+POS_A, POS_B, POS, NEG, TOP = 0, 1, 2, 3, 4
+
+FLOPS = 2 * 2 * ROWS * ROWS * FEATURES
+
+
+def tile_crossgenderinfonceloss_pa_k_kernel(tc, anchor, pos, out):
+    nc = tc.nc
+    with ExitStack() as ctx:
+        const = ctx.enter_context(tc.tile_pool(name="const", bufs=1))
+        keep = ctx.enter_context(tc.tile_pool(name="keep", bufs=1))
+        raw_pool = ctx.enter_context(tc.tile_pool(name="raw", bufs=LOADS_AHEAD + 1))
+        runs_pool = ctx.enter_context(tc.tile_pool(name="runs", bufs=3))
+        grouped_pool = ctx.enter_context(tc.tile_pool(name="grouped", bufs=3))
+        sum_banks = ctx.enter_context(tc.psum_pool(name="sum_banks", bufs=1))
+        turn_banks = ctx.enter_context(tc.psum_pool(name="turn_banks", bufs=4))
+        ctx.enter_context(tc.manual_schedule())
+
+        sources = [x.rearrange("(i p) k -> p i k", p=P) for x in (anchor, pos)]
+
+        codes = keep.tile([P, 4 * PASSES * HALF], U32, align_bytes=64)
+        scales = keep.tile([P, 4 * PASSES * HALF], U8, align_bytes=64)
+
+        neg_logits = keep.tile([P, ROW_TILES, ROWS], F32)
+        negated = keep.tile([P, 2, ROW_TILES, ROWS], F32)
+        shifts = keep.tile([P, 5, ROW_TILES], F32)
+        sums_pos_a = keep.tile([P, ROW_TILES], F32)
+        sums_pos_b = keep.tile([P, ROW_TILES], F32)
+        sums_neg = keep.tile([P, ROW_TILES], F32)
+
+        def start_load(n):
+            raw = raw_pool.tile([P, HALF_TILES, LOAD_FEATURES], BF16)
+            phase, part = divmod(n, LOADS)
+            tiles = slice((phase % 2) * HALF_TILES, (phase % 2 + 1) * HALF_TILES)
+            pieces = LOAD_PASSES if n == 0 else 1
+            width = LOAD_FEATURES // pieces
+            for piece in range(pieces):
+                feature = part * LOAD_FEATURES + piece * width
+                nc.sync.dma_start(
+                    out=raw[:, :, piece * width : (piece + 1) * width],
+                    in_=sources[phase // 2][:, tiles, feature : feature + width],
+                )
+            return raw
+
+        def sort_words(n, raw):
+            runs = runs_pool.tile([P, HALF_TILES * LOAD_PASSES, 2, P], F32)
+            raw_words = raw[:].rearrange("p t k -> p (t k)").bitcast(F32)
+            if n == 0:
+                source = raw_words.rearrange("p (t g b u q) -> p t g u b q", t=HALF_TILES, g=LOAD_PASSES, u=2, q=8)
+                target = runs[:].rearrange("p (t g) u (b q) -> p t g u b q", t=HALF_TILES, q=8)
+                for g in range(LOAD_PASSES):
+                    for u in range(2):
+                        nc.vector.tensor_copy(out=target[:, :, g, u], in_=source[:, :, g, u])
+            else:
+                source = raw_words.rearrange("p (m b u q) -> p m u b q", m=HALF_TILES * LOAD_PASSES, u=2, q=8)
+                target = runs[:].rearrange("p m u (b q) -> p m u b q", q=8)
+                for u in range(2):
+                    nc.vector.tensor_copy(out=target[:, :, u], in_=source[:, :, u])
+            return runs
+
+        def transpose_load(runs):
+            grouped = grouped_pool.tile([P, LOAD_PASSES, HALF, PACK], BF16, align_bytes=64)
+            grouped_words = grouped[:].bitcast(F32)
+            for g in range(LOAD_PASSES):
+                bank = turn_banks.tile([P, 2, HALF], F32)
+                for u in range(2):
+                    for t in range(HALF_TILES):
+                        nc.tensor.transpose(bank[:, u, t * P : (t + 1) * P], runs[:, t * LOAD_PASSES + g, u, :], identity[:])
+                nc.scalar.copy(out=grouped_words[:, g], in_=bank[:].rearrange("q u r -> q r u"))
+            return grouped
+
+        def quantise_load(n, grouped):
+            for g in range(0, LOAD_PASSES, 2):
+                first = (n * LOAD_PASSES + g) * HALF
+                columns = slice(first, first + 2 * HALF)
+                nc.vector.quantize_mx(
+                    out=codes[:, columns].bitcast(FP8X4),
+                    scales=scales[:, columns],
+                    in_=grouped[:, g : g + 2].rearrange("q g r t -> q (g r t)"),
+                )
+
+        def new_sums():
+            return [sum_banks.tile([P, ROWS], F32, name="sum%d" % i, tag="sum%d" % i) for i in range(ROW_TILES)]
+
+        PARTS = [
+            [(0, 0), (1, P)],
+            [(0, 0), (1, 0), (2, 0), (3, P)],
+            [(i, 0) for i in range(ROW_TILES)],
+            [(i, 0) for i in range(ROW_TILES)],
+        ]
+
+        def multiply_load(n, banks):
+            phase, part = divmod(n, LOADS)
+            for i, left in PARTS[phase]:
+                for g in range(LOAD_PASSES):
+                    c = part * LOAD_PASSES + g
+                    first = ((i // HALF_TILES) * PASSES + c) * HALF + (i % HALF_TILES) * P
+                    stationary = slice(first, first + P)
+                    first = (phase * PASSES + c) * HALF
+                    moving = slice(first + left, first + HALF)
+                    nc.tensor.matmul_mx(
+                        out=banks[i][:, left:HALF],
+                        lhsT=codes[:, stationary].bitcast(FP8X4),
+                        lhsT_scale=scales[:, stationary],
+                        rhs=codes[:, moving].bitcast(FP8X4),
+                        rhs_scale=scales[:, moving],
+                        start=(c == 0),
+                        stop=(c == PASSES - 1),
+                    )
+
+        def masked_copy(i, bank, left):
+            nc.vector.tensor_add(out=neg_logits[:, i, i * P : (i + 1) * P], in0=bank[:, left : left + P], in1=masked_diagonal[:])
+
+        def negate(which, first, i, logits, width, slot):
+            nc.vector.tensor_scalar(
+                out=negated[:, which, i, first : first + width],
+                in0=logits,
+                scalar1=-1.0 / TEMPERATURE,
+                scalar2=None,
+                op0=ALU.mult,
+                op1=ALU.min,
+                accum_out=shifts[:, slot, i : i + 1],
+            )
+
+        def exponentials(which, first, i, width, slot, sums):
+            nc.scalar.activation(
+                out=negated[:, which, i, first : first + width],
+                in_=negated[:, which, i, first : first + width],
+                func=ACT.Exp,
+                bias=shifts[:, slot, i : i + 1],
+                scale=-1.0,
+                accum_out=sums[:, i : i + 1],
+            )
+
+        raws = {}
+        for n in range(LOADS_AHEAD):
+            raws[n] = start_load(n)
+
+        identity = const.tile([P, P], F32)
+        masks.make_identity(nc, identity[:])
+        masked_diagonal = const.tile([P, P], F32)
+        nc.vector.tensor_scalar_mul(out=masked_diagonal[:], in0=identity[:], scalar1=MASKED)
+        final = keep.tile([P, 2, P], F32)
+        nc.vector.memset(final[:], 0.0)
+        warm = const.tile([P, 1], F32)
+        nc.vector.memset(warm[:], 0.0)
+        nc.scalar.activation(out=warm[:], in_=warm[:], func=ACT.Exp)
+
+        runs = {0: sort_words(0, raws[0])}
+        banks = new_sums()
+        for n in range(ALL_LOADS):
+            if n + LOADS_AHEAD < ALL_LOADS:
+                raws[n + LOADS_AHEAD] = start_load(n + LOADS_AHEAD)
+            if n + 1 < ALL_LOADS:
+                runs[n + 1] = sort_words(n + 1, raws[n + 1])
+            grouped = transpose_load(runs[n])
+            if n == 10:
+                lower = turn_banks.tile([P, ROWS], F32, name="lower", tag="bank")
+                middle = turn_banks.tile([P, ROWS], F32, name="middle", tag="bank")
+                for bank, column, i, j in ((lower, 0, 1, 0), (middle, 0, 2, 0), (middle, 1, 2, 1), (lower, 1, 3, 0), (lower, 2, 3, 1), (lower, 3, 3, 2)):
+                    nc.tensor.transpose(bank[:, column * P : (column + 1) * P], neg_logits[:, j, i * P : (i + 1) * P], identity[:])
+                nc.scalar.copy(out=neg_logits[:, 1, :P], in_=lower[:, :P])
+                nc.scalar.copy(out=neg_logits[:, 3, : 3 * P], in_=lower[:, P:])
+                nc.scalar.copy(out=neg_logits[:, 2, :HALF], in_=middle[:, :HALF])
+            if n > 0:
+                multiply_load(n - 1, banks)
+            quantise_load(n, grouped)
+            if n == LOADS:
+                masked_copy(0, banks[0], 0)
+                masked_copy(1, banks[1], P)
+                nc.scalar.copy(out=neg_logits[:, 0, P:HALF], in_=banks[0][:, P:HALF])
+                banks = new_sums()
+            if n == 2 * LOADS:
+                masked_copy(2, banks[2], 0)
+                masked_copy(3, banks[3], P)
+                nc.scalar.copy(out=neg_logits[:, 0, HALF:], in_=banks[0][:, :HALF])
+                nc.scalar.copy(out=neg_logits[:, 1, HALF:], in_=banks[1][:, :HALF])
+                nc.scalar.copy(out=neg_logits[:, 2, 3 * P :], in_=banks[2][:, P:HALF])
+                banks = new_sums()
+            if n == 9:
+                negate(1, 0, 0, neg_logits[:, 0, :], ROWS, NEG)
+                exponentials(1, 0, 0, ROWS, NEG, sums_neg)
+            if n in (10, 11):
+                negate(1, 0, n - 9, neg_logits[:, n - 9, :], ROWS, NEG)
+                exponentials(1, 0, n - 9, ROWS, NEG, sums_neg)
+            if n == 12:
+                for i in range(ROW_TILES):
+                    negate(0, 0, i, banks[i][:, :HALF], HALF, POS_A)
+                banks = new_sums()
+                for i in range(ROW_TILES):
+                    exponentials(0, 0, i, HALF, POS_A, sums_pos_a)
+            if n == 13:
+                negate(1, 0, 3, neg_logits[:, 3, :], ROWS, NEG)
+                exponentials(1, 0, 3, ROWS, NEG, sums_neg)
+        multiply_load(ALL_LOADS - 1, banks)
+        for i in range(ROW_TILES):
+            negate(0, HALF, i, banks[i][:, :HALF], HALF, POS_B)
+            exponentials(0, HALF, i, HALF, POS_B, sums_pos_b)
+
+        gaps = keep.tile([P, 4, ROW_TILES], F32)
+        weights = keep.tile([P, 4, ROW_TILES], F32)
+        part_a = keep.tile([P, ROW_TILES], F32)
+        part_b = keep.tile([P, ROW_TILES], F32)
+        total_pos = keep.tile([P, ROW_TILES], F32)
+        total_neg = keep.tile([P, ROW_TILES], F32)
+        inverse = keep.tile([P, ROW_TILES], F32)
+        ratio = keep.tile([P, ROW_TILES], F32)
+        nc.vector.tensor_tensor(out=shifts[:, POS, :], in0=shifts[:, POS_A, :], in1=shifts[:, POS_B, :], op=ALU.min)
+        nc.vector.tensor_tensor(out=shifts[:, TOP, :], in0=shifts[:, POS, :], in1=shifts[:, NEG, :], op=ALU.min)
+        nc.vector.tensor_sub(
+            out=gaps[:].rearrange("p (a b) i -> p a b i", a=2),
+            in0=shifts[:, POS : TOP + 1 : 2, :].unsqueeze(2).to_broadcast([P, 2, 2, ROW_TILES]),
+            in1=shifts[:, :TOP, :].rearrange("p (a b) i -> p a b i", a=2),
+        )
+        nc.scalar.activation(out=weights[:], in_=gaps[:], func=ACT.Exp)
+        nc.scalar.activation(out=warm[:], in_=warm[:], func=ACT.Ln)
+        nc.vector.tensor_copy(out=final[:, 1, :ROW_TILES], in_=gaps[:, POS, :])
+        nc.vector.tensor_mul(out=part_a[:], in0=sums_pos_a[:], in1=weights[:, POS_A, :])
+        nc.vector.tensor_mul(out=total_neg[:], in0=sums_neg[:], in1=weights[:, NEG, :])
+        nc.vector.tensor_mul(out=part_b[:], in0=sums_pos_b[:], in1=weights[:, POS_B, :])
+        nc.vector.tensor_add(out=total_pos[:], in0=part_a[:], in1=part_b[:])
+        nc.vector.reciprocal(out=inverse[:], in_=total_pos[:])
+        nc.vector.tensor_mul(out=ratio[:], in0=total_neg[:], in1=inverse[:])
+        nc.vector.tensor_add(out=final[:, 0, :ROW_TILES], in0=ratio[:], in1=weights[:, POS, :])
+        turned = turn_banks.tile([P, 2, P], F32, name="turned", tag="bank")
+        nc.tensor.transpose(turned[:, 1, :], final[:, 1, :], identity[:])
+        nc.tensor.transpose(turned[:, 0, :], final[:, 0, :], identity[:])
+        logs = keep.tile([P, P], F32)
+        results = keep.tile([P, P], F32)
+        nc.scalar.activation(out=logs[:ROW_TILES, :], in_=turned[:ROW_TILES, 0, :], func=ACT.Ln)
+        nc.vector.tensor_sub(out=results[:ROW_TILES, :], in0=turned[:ROW_TILES, 1, :], in1=logs[:ROW_TILES, :])
+        nc.sync.dma_start(out=out.rearrange("(i p) -> i p", p=P), in_=results[:ROW_TILES, :])

@@ -14,21 +14,23 @@ ALU = mybir.AluOpType
 P = 128
 PACK = 4
 K_PASS = P * PACK
-BLOCKS = K_PASS // 32
 ROWS = 512
 ROW_TILES = ROWS // P
 HALF = ROWS // 2
-HALF_TILES = HALF // P
 FEATURES = 8192
 PASSES = FEATURES // K_PASS
-LOAD_PASSES = 4
-LOAD_FEATURES = LOAD_PASSES * K_PASS
-LOADS = FEATURES // LOAD_FEATURES
-ALL_LOADS = 4 * LOADS
+BANKS = 4
+BANK_TILES = 2
+COLUMNS = BANKS * HALF
+LOADS = PASSES * ROWS // COLUMNS
+HALF_LOADS = LOADS // 2
+ALL_LOADS = 2 * LOADS
 LOADS_AHEAD = 6
+FINE_LOADS = 2
 TEMPERATURE = 0.07
 MASKED = -1.0e30
-POS_A, POS_B, POS, NEG, TOP = 0, 1, 2, 3, 4
+POS_A, POS, NEG = 0, 1, 2
+WARM_MATMULS = 5
 
 FLOPS = 2 * 2 * ROWS * ROWS * FEATURES
 
@@ -42,93 +44,110 @@ def tile_crossgenderinfonceloss_pa_k_kernel(tc, anchor, pos, out):
         runs_pool = ctx.enter_context(tc.tile_pool(name="runs", bufs=3))
         grouped_pool = ctx.enter_context(tc.tile_pool(name="grouped", bufs=3))
         sum_banks = ctx.enter_context(tc.psum_pool(name="sum_banks", bufs=1))
-        turn_banks = ctx.enter_context(tc.psum_pool(name="turn_banks", bufs=4))
+        turn_banks = ctx.enter_context(tc.psum_pool(name="turn_banks", bufs=BANKS))
         ctx.enter_context(tc.manual_schedule())
 
         sources = [x.rearrange("(i p) k -> p i k", p=P) for x in (anchor, pos)]
 
-        codes = keep.tile([P, 4 * PASSES * HALF], U32, align_bytes=64)
-        scales = keep.tile([P, 4 * PASSES * HALF], U8, align_bytes=64)
+        codes = keep.tile([P, ALL_LOADS * COLUMNS], U32, align_bytes=64)
+        scales = keep.tile([P, ALL_LOADS * COLUMNS], U8, align_bytes=64)
 
         neg_logits = keep.tile([P, ROW_TILES, ROWS], F32)
         negated = keep.tile([P, 2, ROW_TILES, ROWS], F32)
-        shifts = keep.tile([P, 5, ROW_TILES], F32)
-        sums_pos_a = keep.tile([P, ROW_TILES], F32)
-        sums_pos_b = keep.tile([P, ROW_TILES], F32)
-        sums_neg = keep.tile([P, ROW_TILES], F32)
+        shifts = keep.tile([P, 3, ROW_TILES], F32)
+        sums = keep.tile([P, 3, ROW_TILES], F32)
+
+        def shape_of(n):
+            tiles = ROW_TILES if n < LOADS else BANK_TILES
+            return tiles, BANKS * BANK_TILES // tiles
+
+        def pieces_of(n):
+            tiles, passes = shape_of(n)
+            halves = [(0, 0, BANK_TILES), (0, BANK_TILES, BANK_TILES)] if n == 0 else [(0, 0, tiles)]
+            return halves + [(g, 0, tiles) for g in range(1, passes)]
 
         def start_load(n):
-            raw = raw_pool.tile([P, HALF_TILES, LOAD_FEATURES], BF16)
-            phase, part = divmod(n, LOADS)
-            tiles = slice((phase % 2) * HALF_TILES, (phase % 2 + 1) * HALF_TILES)
-            pieces = LOAD_PASSES if n == 0 else 1
-            width = LOAD_FEATURES // pieces
-            for piece in range(pieces):
-                feature = part * LOAD_FEATURES + piece * width
+            tiles, passes = shape_of(n)
+            features = passes * K_PASS
+            raw = raw_pool.tile([P, tiles, features], BF16)
+            if n < FINE_LOADS:
+                for g, t, width in pieces_of(n):
+                    nc.sync.dma_start(
+                        out=raw[:, t : t + width, g * K_PASS : (g + 1) * K_PASS],
+                        in_=sources[0][:, t : t + width, n * features + g * K_PASS : n * features + (g + 1) * K_PASS],
+                    )
+            elif n < LOADS:
+                nc.sync.dma_start(out=raw[:], in_=sources[0][:, :, n * features : (n + 1) * features])
+            else:
+                half, part = divmod(n - LOADS, HALF_LOADS)
                 nc.sync.dma_start(
-                    out=raw[:, :, piece * width : (piece + 1) * width],
-                    in_=sources[phase // 2][:, tiles, feature : feature + width],
+                    out=raw[:],
+                    in_=sources[1][:, half * BANK_TILES : (half + 1) * BANK_TILES, part * features : (part + 1) * features],
                 )
             return raw
 
-        def sort_words(n, raw):
-            runs = runs_pool.tile([P, HALF_TILES * LOAD_PASSES, 2, P], F32)
+        def new_runs():
+            return runs_pool.tile([P, BANKS * BANK_TILES, 2, P], F32, name="runs")
+
+        def sort_words(n, raw, runs, chosen):
+            tiles, passes = shape_of(n)
             raw_words = raw[:].rearrange("p t k -> p (t k)").bitcast(F32)
-            if n == 0:
-                source = raw_words.rearrange("p (t g b u q) -> p t g u b q", t=HALF_TILES, g=LOAD_PASSES, u=2, q=8)
-                target = runs[:].rearrange("p (t g) u (b q) -> p t g u b q", t=HALF_TILES, q=8)
-                for g in range(LOAD_PASSES):
-                    for u in range(2):
-                        nc.vector.tensor_copy(out=target[:, :, g, u], in_=source[:, :, g, u])
+            if n < FINE_LOADS:
+                source = raw_words.rearrange("p (t g b u q) -> p t g u b q", t=tiles, g=passes, u=2, q=8)
+                target = runs[:].rearrange("p (t g) u (b q) -> p t g u b q", t=tiles, q=8)
+                for g, t, width in pieces_of(n):
+                    if g in chosen:
+                        for u in range(2):
+                            nc.vector.tensor_copy(out=target[:, t : t + width, g, u], in_=source[:, t : t + width, g, u])
             else:
-                source = raw_words.rearrange("p (m b u q) -> p m u b q", m=HALF_TILES * LOAD_PASSES, u=2, q=8)
+                source = raw_words.rearrange("p (m b u q) -> p m u b q", m=tiles * passes, u=2, q=8)
                 target = runs[:].rearrange("p m u (b q) -> p m u b q", q=8)
                 for u in range(2):
                     nc.vector.tensor_copy(out=target[:, :, u], in_=source[:, :, u])
-            return runs
 
-        def transpose_load(runs):
-            grouped = grouped_pool.tile([P, LOAD_PASSES, HALF, PACK], BF16, align_bytes=64)
+        def new_grouped():
+            return grouped_pool.tile([P, COLUMNS, PACK], BF16, align_bytes=64, name="grouped")
+
+        def transpose_load(n, runs, grouped, chosen):
+            tiles, passes = shape_of(n)
             grouped_words = grouped[:].bitcast(F32)
-            for g in range(LOAD_PASSES):
+            for k in range(BANKS):
+                g, first = divmod(k * BANK_TILES, tiles)
+                if g not in chosen:
+                    continue
                 bank = turn_banks.tile([P, 2, HALF], F32)
                 for u in range(2):
-                    for t in range(HALF_TILES):
-                        nc.tensor.transpose(bank[:, u, t * P : (t + 1) * P], runs[:, t * LOAD_PASSES + g, u, :], identity[:])
-                nc.scalar.copy(out=grouped_words[:, g], in_=bank[:].rearrange("q u r -> q r u"))
-            return grouped
+                    for j in range(BANK_TILES):
+                        nc.tensor.transpose(bank[:, u, j * P : (j + 1) * P], runs[:, (first + j) * passes + g, u, :], identity[:])
+                nc.scalar.copy(out=grouped_words[:, k * HALF : (k + 1) * HALF], in_=bank[:].rearrange("q u r -> q r u"))
 
-        def quantise_load(n, grouped):
-            for g in range(0, LOAD_PASSES, 2):
-                first = (n * LOAD_PASSES + g) * HALF
-                columns = slice(first, first + 2 * HALF)
+        def quantise_load(n, grouped, chosen):
+            tiles, passes = shape_of(n)
+            for first in range(chosen[0] * tiles * P, (chosen[-1] + 1) * tiles * P, ROWS):
+                columns = slice(n * COLUMNS + first, n * COLUMNS + first + ROWS)
                 nc.vector.quantize_mx(
                     out=codes[:, columns].bitcast(FP8X4),
                     scales=scales[:, columns],
-                    in_=grouped[:, g : g + 2].rearrange("q g r t -> q (g r t)"),
+                    in_=grouped[:, first : first + ROWS].rearrange("q c t -> q (c t)"),
                 )
 
         def new_sums():
             return [sum_banks.tile([P, ROWS], F32, name="sum%d" % i, tag="sum%d" % i) for i in range(ROW_TILES)]
 
-        PARTS = [
-            [(0, 0), (1, P)],
-            [(0, 0), (1, 0), (2, 0), (3, P)],
-            [(i, 0) for i in range(ROW_TILES)],
-            [(i, 0) for i in range(ROW_TILES)],
-        ]
+        LEFT = [0, 0, 2 * P, 3 * P]
 
-        def multiply_load(n, banks):
-            phase, part = divmod(n, LOADS)
-            for i, left in PARTS[phase]:
-                for g in range(LOAD_PASSES):
-                    c = part * LOAD_PASSES + g
-                    first = ((i // HALF_TILES) * PASSES + c) * HALF + (i % HALF_TILES) * P
-                    stationary = slice(first, first + P)
-                    first = (phase * PASSES + c) * HALF
-                    moving = slice(first + left, first + HALF)
+        def multiply_load(n, banks, chosen):
+            tiles, passes = shape_of(n)
+            rows = tiles * P
+            for i in range(ROW_TILES):
+                left = LEFT[i] if n < LOADS else 0
+                for g in chosen:
+                    c = (n if n < LOADS else (n - LOADS) % HALF_LOADS) * passes + g
+                    stationary = slice(c * ROWS + i * P, c * ROWS + (i + 1) * P)
+                    first = n * COLUMNS + g * rows
+                    moving = slice(first + left, first + rows)
                     nc.tensor.matmul_mx(
-                        out=banks[i][:, left:HALF],
+                        out=banks[i][:, left:rows],
                         lhsT=codes[:, stationary].bitcast(FP8X4),
                         lhsT_scale=scales[:, stationary],
                         rhs=codes[:, moving].bitcast(FP8X4),
@@ -137,28 +156,25 @@ def tile_crossgenderinfonceloss_pa_k_kernel(tc, anchor, pos, out):
                         stop=(c == PASSES - 1),
                     )
 
-        def masked_copy(i, bank, left):
-            nc.vector.tensor_add(out=neg_logits[:, i, i * P : (i + 1) * P], in0=bank[:, left : left + P], in1=masked_diagonal[:])
-
-        def negate(which, first, i, logits, width, slot):
+        def negate(which, first, i, logits, width, slot, start=None):
             nc.vector.tensor_scalar(
                 out=negated[:, which, i, first : first + width],
                 in0=logits,
                 scalar1=-1.0 / TEMPERATURE,
-                scalar2=None,
+                scalar2=start,
                 op0=ALU.mult,
                 op1=ALU.min,
                 accum_out=shifts[:, slot, i : i + 1],
             )
 
-        def exponentials(which, first, i, width, slot, sums):
+        def exponentials(which, first, i, width, slot):
             nc.scalar.activation(
                 out=negated[:, which, i, first : first + width],
                 in_=negated[:, which, i, first : first + width],
                 func=ACT.Exp,
                 bias=shifts[:, slot, i : i + 1],
                 scale=-1.0,
-                accum_out=sums[:, i : i + 1],
+                accum_out=sums[:, slot, i : i + 1],
             )
 
         raws = {}
@@ -174,82 +190,94 @@ def tile_crossgenderinfonceloss_pa_k_kernel(tc, anchor, pos, out):
         warm = const.tile([P, 1], F32)
         nc.vector.memset(warm[:], 0.0)
         nc.scalar.activation(out=warm[:], in_=warm[:], func=ACT.Exp)
-
-        runs = {0: sort_words(0, raws[0])}
+        idle = const.tile([P, ROWS], BF16)
+        nc.vector.memset(idle[:], 0.0)
         banks = new_sums()
-        for n in range(ALL_LOADS):
-            if n + LOADS_AHEAD < ALL_LOADS:
-                raws[n + LOADS_AHEAD] = start_load(n + LOADS_AHEAD)
-            if n + 1 < ALL_LOADS:
-                runs[n + 1] = sort_words(n + 1, raws[n + 1])
-            grouped = transpose_load(runs[n])
-            if n == 10:
+        for k in range(WARM_MATMULS):
+            nc.tensor.matmul(banks[3][:], lhsT=idle[:, :P], rhs=idle[:], start=True, stop=True)
+
+        steps = [(n, [g]) for n in range(FINE_LOADS) for g in range(shape_of(n)[1])]
+        steps += [(n, list(range(shape_of(n)[1]))) for n in range(FINE_LOADS, ALL_LOADS)]
+        runs = {}
+        groups = {}
+
+        def sort_step(s):
+            n, chosen = steps[s]
+            if n not in runs:
+                runs[n] = new_runs()
+            sort_words(n, raws[n], runs[n], chosen)
+
+        sort_step(0)
+        for s in range(len(steps)):
+            n, chosen = steps[s]
+            if chosen[0] == 0:
+                groups[n] = new_grouped()
+                if n + LOADS_AHEAD < ALL_LOADS:
+                    raws[n + LOADS_AHEAD] = start_load(n + LOADS_AHEAD)
+            if s + 1 < len(steps):
+                sort_step(s + 1)
+            transpose_load(n, runs[n], groups[n], chosen)
+            if n == LOADS + 2:
                 lower = turn_banks.tile([P, ROWS], F32, name="lower", tag="bank")
                 middle = turn_banks.tile([P, ROWS], F32, name="middle", tag="bank")
-                for bank, column, i, j in ((lower, 0, 1, 0), (middle, 0, 2, 0), (middle, 1, 2, 1), (lower, 1, 3, 0), (lower, 2, 3, 1), (lower, 3, 3, 2)):
-                    nc.tensor.transpose(bank[:, column * P : (column + 1) * P], neg_logits[:, j, i * P : (i + 1) * P], identity[:])
-                nc.scalar.copy(out=neg_logits[:, 1, :P], in_=lower[:, :P])
-                nc.scalar.copy(out=neg_logits[:, 3, : 3 * P], in_=lower[:, P:])
-                nc.scalar.copy(out=neg_logits[:, 2, :HALF], in_=middle[:, :HALF])
-            if n > 0:
-                multiply_load(n - 1, banks)
-            quantise_load(n, grouped)
+                for bank, i in ((middle, 2), (lower, 3)):
+                    for j in range(i):
+                        nc.tensor.transpose(bank[:, j * P : (j + 1) * P], neg_logits[:, j, i * P : (i + 1) * P], identity[:])
+                    nc.scalar.copy(out=neg_logits[:, i, : i * P], in_=bank[:, : i * P])
+            if s > 0:
+                multiply_load(steps[s - 1][0], banks, steps[s - 1][1])
+            quantise_load(n, groups[n], chosen)
             if n == LOADS:
-                masked_copy(0, banks[0], 0)
-                masked_copy(1, banks[1], P)
-                nc.scalar.copy(out=neg_logits[:, 0, P:HALF], in_=banks[0][:, P:HALF])
+                for i in range(ROW_TILES):
+                    block = slice(i * P, (i + 1) * P)
+                    nc.vector.tensor_add(out=neg_logits[:, i, block], in0=banks[i][:, block], in1=masked_diagonal[:])
+                nc.scalar.copy(out=neg_logits[:, 0, P:], in_=banks[0][:, P:])
+                nc.scalar.copy(out=neg_logits[:, 1, :P], in_=banks[1][:, :P])
+                nc.scalar.copy(out=neg_logits[:, 1, HALF:], in_=banks[1][:, HALF:])
+                nc.scalar.copy(out=neg_logits[:, 2, 3 * P :], in_=banks[2][:, 3 * P :])
                 banks = new_sums()
-            if n == 2 * LOADS:
-                masked_copy(2, banks[2], 0)
-                masked_copy(3, banks[3], P)
-                nc.scalar.copy(out=neg_logits[:, 0, HALF:], in_=banks[0][:, :HALF])
-                nc.scalar.copy(out=neg_logits[:, 1, HALF:], in_=banks[1][:, :HALF])
-                nc.scalar.copy(out=neg_logits[:, 2, 3 * P :], in_=banks[2][:, P:HALF])
-                banks = new_sums()
-            if n == 9:
-                negate(1, 0, 0, neg_logits[:, 0, :], ROWS, NEG)
-                exponentials(1, 0, 0, ROWS, NEG, sums_neg)
-            if n in (10, 11):
-                negate(1, 0, n - 9, neg_logits[:, n - 9, :], ROWS, NEG)
-                exponentials(1, 0, n - 9, ROWS, NEG, sums_neg)
-            if n == 12:
+            i = n - (LOADS + 2)
+            if i in (0, 1):
+                negate(1, 0, i, neg_logits[:, i, :], ROWS, NEG)
+            if i in (3, 4):
+                negate(1, 0, i - 1, neg_logits[:, i - 1, :], ROWS, NEG)
+            if i in (1, 2):
+                exponentials(1, 0, i - 1, ROWS, NEG)
+            if i in (4, 5):
+                exponentials(1, 0, i - 2, ROWS, NEG)
+            if n == LOADS + HALF_LOADS:
                 for i in range(ROW_TILES):
                     negate(0, 0, i, banks[i][:, :HALF], HALF, POS_A)
                 banks = new_sums()
-                for i in range(ROW_TILES):
-                    exponentials(0, 0, i, HALF, POS_A, sums_pos_a)
-            if n == 13:
-                negate(1, 0, 3, neg_logits[:, 3, :], ROWS, NEG)
-                exponentials(1, 0, 3, ROWS, NEG, sums_neg)
-        multiply_load(ALL_LOADS - 1, banks)
+            if n in (LOADS + HALF_LOADS + 1, LOADS + HALF_LOADS + 3):
+                for i in (n - LOADS - HALF_LOADS - 1, n - LOADS - HALF_LOADS):
+                    exponentials(0, 0, i, HALF, POS_A)
+        multiply_load(steps[-1][0], banks, steps[-1][1])
         for i in range(ROW_TILES):
-            negate(0, HALF, i, banks[i][:, :HALF], HALF, POS_B)
-            exponentials(0, HALF, i, HALF, POS_B, sums_pos_b)
+            negate(0, HALF, i, banks[i][:, :HALF], HALF, POS, shifts[:, POS_A, i : i + 1])
+            exponentials(0, HALF, i, HALF, POS)
 
-        gaps = keep.tile([P, 4, ROW_TILES], F32)
-        weights = keep.tile([P, 4, ROW_TILES], F32)
-        part_a = keep.tile([P, ROW_TILES], F32)
-        part_b = keep.tile([P, ROW_TILES], F32)
+        gaps = keep.tile([P, 3, ROW_TILES], F32)
+        weights = keep.tile([P, 3, ROW_TILES], F32)
+        weighted = keep.tile([P, 2, ROW_TILES], F32)
+        minus_top = keep.tile([P, ROW_TILES], F32)
         total_pos = keep.tile([P, ROW_TILES], F32)
-        total_neg = keep.tile([P, ROW_TILES], F32)
         inverse = keep.tile([P, ROW_TILES], F32)
         ratio = keep.tile([P, ROW_TILES], F32)
-        nc.vector.tensor_tensor(out=shifts[:, POS, :], in0=shifts[:, POS_A, :], in1=shifts[:, POS_B, :], op=ALU.min)
-        nc.vector.tensor_tensor(out=shifts[:, TOP, :], in0=shifts[:, POS, :], in1=shifts[:, NEG, :], op=ALU.min)
+        nc.vector.tensor_tensor(out=minus_top[:], in0=shifts[:, POS, :], in1=shifts[:, NEG, :], op=ALU.min)
+        nc.vector.tensor_sub(out=gaps[:, POS_A, :], in0=shifts[:, POS, :], in1=shifts[:, POS_A, :])
         nc.vector.tensor_sub(
-            out=gaps[:].rearrange("p (a b) i -> p a b i", a=2),
-            in0=shifts[:, POS : TOP + 1 : 2, :].unsqueeze(2).to_broadcast([P, 2, 2, ROW_TILES]),
-            in1=shifts[:, :TOP, :].rearrange("p (a b) i -> p a b i", a=2),
+            out=gaps[:, POS:, :],
+            in0=minus_top[:].unsqueeze(1).to_broadcast([P, 2, ROW_TILES]),
+            in1=shifts[:, POS:, :],
         )
         nc.scalar.activation(out=weights[:], in_=gaps[:], func=ACT.Exp)
         nc.scalar.activation(out=warm[:], in_=warm[:], func=ACT.Ln)
         nc.vector.tensor_copy(out=final[:, 1, :ROW_TILES], in_=gaps[:, POS, :])
-        nc.vector.tensor_mul(out=part_a[:], in0=sums_pos_a[:], in1=weights[:, POS_A, :])
-        nc.vector.tensor_mul(out=total_neg[:], in0=sums_neg[:], in1=weights[:, NEG, :])
-        nc.vector.tensor_mul(out=part_b[:], in0=sums_pos_b[:], in1=weights[:, POS_B, :])
-        nc.vector.tensor_add(out=total_pos[:], in0=part_a[:], in1=part_b[:])
+        nc.vector.tensor_mul(out=weighted[:], in0=sums[:, POS_A : NEG + 1 : 2, :], in1=weights[:, POS_A : NEG + 1 : 2, :])
+        nc.vector.tensor_add(out=total_pos[:], in0=weighted[:, 0, :], in1=sums[:, POS, :])
         nc.vector.reciprocal(out=inverse[:], in_=total_pos[:])
-        nc.vector.tensor_mul(out=ratio[:], in0=total_neg[:], in1=inverse[:])
+        nc.vector.tensor_mul(out=ratio[:], in0=weighted[:, 1, :], in1=inverse[:])
         nc.vector.tensor_add(out=final[:, 0, :ROW_TILES], in0=ratio[:], in1=weights[:, POS, :])
         turned = turn_banks.tile([P, 2, P], F32, name="turned", tag="bank")
         nc.tensor.transpose(turned[:, 1, :], final[:, 1, :], identity[:])

@@ -31,6 +31,7 @@ TEMPERATURE = 0.07
 MASKED = -1.0e30
 POS_A, POS, NEG = 0, 1, 2
 WARM_MATMULS = 5
+FILLED_STEPS = 2
 
 FLOPS = 2 * 2 * ROWS * ROWS * FEATURES
 
@@ -134,7 +135,7 @@ def tile_crossgenderinfonceloss_pa_k_kernel(tc, anchor, pos, out):
         def new_sums():
             return [sum_banks.tile([P, ROWS], F32, name="sum%d" % i, tag="sum%d" % i) for i in range(ROW_TILES)]
 
-        LEFT = [0, 0, 2 * P, 3 * P]
+        LEFT = [0, 2 * P, 2 * P, 3 * P]
 
         def multiply_load(n, banks, chosen):
             tiles, passes = shape_of(n)
@@ -155,6 +156,19 @@ def tile_crossgenderinfonceloss_pa_k_kernel(tc, anchor, pos, out):
                         start=(c == 0),
                         stop=(c == PASSES - 1),
                     )
+
+        def multiply_middle(bank):
+            for c in range(PASSES):
+                block = slice(c * ROWS + P, c * ROWS + 2 * P)
+                nc.tensor.matmul_mx(
+                    out=bank[:, :P],
+                    lhsT=codes[:, block].bitcast(FP8X4),
+                    lhsT_scale=scales[:, block],
+                    rhs=codes[:, block].bitcast(FP8X4),
+                    rhs_scale=scales[:, block],
+                    start=(c == 0),
+                    stop=(c == PASSES - 1),
+                )
 
         def negate(which, first, i, logits, width, slot, start=None):
             nc.vector.tensor_scalar(
@@ -193,8 +207,12 @@ def tile_crossgenderinfonceloss_pa_k_kernel(tc, anchor, pos, out):
         idle = const.tile([P, ROWS], BF16)
         nc.vector.memset(idle[:], 0.0)
         banks = new_sums()
-        for k in range(WARM_MATMULS):
+
+        def warm_up():
             nc.tensor.matmul(banks[3][:], lhsT=idle[:, :P], rhs=idle[:], start=True, stop=True)
+
+        for k in range(WARM_MATMULS):
+            warm_up()
 
         steps = [(n, [g]) for n in range(FINE_LOADS) for g in range(shape_of(n)[1])]
         steps += [(n, list(range(shape_of(n)[1]))) for n in range(FINE_LOADS, ALL_LOADS)]
@@ -217,22 +235,25 @@ def tile_crossgenderinfonceloss_pa_k_kernel(tc, anchor, pos, out):
             if s + 1 < len(steps):
                 sort_step(s + 1)
             transpose_load(n, runs[n], groups[n], chosen)
+            if s < FILLED_STEPS:
+                warm_up()
             if n == LOADS + 2:
                 lower = turn_banks.tile([P, ROWS], F32, name="lower", tag="bank")
                 middle = turn_banks.tile([P, ROWS], F32, name="middle", tag="bank")
-                for bank, i in ((middle, 2), (lower, 3)):
+                for bank, i, place in ((middle, 1, 3 * P), (middle, 2, 0), (lower, 3, 0)):
                     for j in range(i):
-                        nc.tensor.transpose(bank[:, j * P : (j + 1) * P], neg_logits[:, j, i * P : (i + 1) * P], identity[:])
-                    nc.scalar.copy(out=neg_logits[:, i, : i * P], in_=bank[:, : i * P])
+                        nc.tensor.transpose(bank[:, place + j * P : place + (j + 1) * P], neg_logits[:, j, i * P : (i + 1) * P], identity[:])
+                    nc.scalar.copy(out=neg_logits[:, i, : i * P], in_=bank[:, place : place + i * P])
             if s > 0:
                 multiply_load(steps[s - 1][0], banks, steps[s - 1][1])
             quantise_load(n, groups[n], chosen)
             if n == LOADS:
-                for i in range(ROW_TILES):
+                multiply_middle(banks[3])
+                for i in (0, 2, 3, 1):
                     block = slice(i * P, (i + 1) * P)
-                    nc.vector.tensor_add(out=neg_logits[:, i, block], in0=banks[i][:, block], in1=masked_diagonal[:])
+                    source = banks[3][:, :P] if i == 1 else banks[i][:, block]
+                    nc.vector.tensor_add(out=neg_logits[:, i, block], in0=source, in1=masked_diagonal[:])
                 nc.scalar.copy(out=neg_logits[:, 0, P:], in_=banks[0][:, P:])
-                nc.scalar.copy(out=neg_logits[:, 1, :P], in_=banks[1][:, :P])
                 nc.scalar.copy(out=neg_logits[:, 1, HALF:], in_=banks[1][:, HALF:])
                 nc.scalar.copy(out=neg_logits[:, 2, 3 * P :], in_=banks[2][:, 3 * P :])
                 banks = new_sums()
@@ -259,11 +280,10 @@ def tile_crossgenderinfonceloss_pa_k_kernel(tc, anchor, pos, out):
 
         gaps = keep.tile([P, 3, ROW_TILES], F32)
         weights = keep.tile([P, 3, ROW_TILES], F32)
-        weighted = keep.tile([P, 2, ROW_TILES], F32)
+        weighted = keep.tile([P, ROW_TILES], F32)
         minus_top = keep.tile([P, ROW_TILES], F32)
         total_pos = keep.tile([P, ROW_TILES], F32)
         inverse = keep.tile([P, ROW_TILES], F32)
-        ratio = keep.tile([P, ROW_TILES], F32)
         nc.vector.tensor_tensor(out=minus_top[:], in0=shifts[:, POS, :], in1=shifts[:, NEG, :], op=ALU.min)
         nc.vector.tensor_sub(out=gaps[:, POS_A, :], in0=shifts[:, POS, :], in1=shifts[:, POS_A, :])
         nc.vector.tensor_sub(
@@ -274,11 +294,28 @@ def tile_crossgenderinfonceloss_pa_k_kernel(tc, anchor, pos, out):
         nc.scalar.activation(out=weights[:], in_=gaps[:], func=ACT.Exp)
         nc.scalar.activation(out=warm[:], in_=warm[:], func=ACT.Ln)
         nc.vector.tensor_copy(out=final[:, 1, :ROW_TILES], in_=gaps[:, POS, :])
-        nc.vector.tensor_mul(out=weighted[:], in0=sums[:, POS_A : NEG + 1 : 2, :], in1=weights[:, POS_A : NEG + 1 : 2, :])
-        nc.vector.tensor_add(out=total_pos[:], in0=weighted[:, 0, :], in1=sums[:, POS, :])
+        nc.vector.tensor_mul(out=weighted[:], in0=sums[:, NEG, :], in1=weights[:, NEG, :])
+        for i in range(ROW_TILES):
+            one = slice(i, i + 1)
+            nc.vector.scalar_tensor_tensor(
+                out=total_pos[:, one],
+                in0=sums[:, POS_A, one],
+                scalar=weights[:, POS_A, one],
+                in1=sums[:, POS, one],
+                op0=ALU.mult,
+                op1=ALU.add,
+            )
         nc.vector.reciprocal(out=inverse[:], in_=total_pos[:])
-        nc.vector.tensor_mul(out=ratio[:], in0=weighted[:, 1, :], in1=inverse[:])
-        nc.vector.tensor_add(out=final[:, 0, :ROW_TILES], in0=ratio[:], in1=weights[:, POS, :])
+        for i in range(ROW_TILES):
+            one = slice(i, i + 1)
+            nc.vector.scalar_tensor_tensor(
+                out=final[:, 0, one],
+                in0=inverse[:, one],
+                scalar=weighted[:, one],
+                in1=weights[:, POS, one],
+                op0=ALU.mult,
+                op1=ALU.add,
+            )
         turned = turn_banks.tile([P, 2, P], F32, name="turned", tag="bank")
         nc.tensor.transpose(turned[:, 1, :], final[:, 1, :], identity[:])
         nc.tensor.transpose(turned[:, 0, :], final[:, 0, :], identity[:])

@@ -240,9 +240,11 @@ def tile_crossgenderinfonceloss_pa_k_kernel(tc, anchor, pos, out):
             if n == LOADS + 2:
                 lower = turn_banks.tile([P, ROWS], F32, name="lower", tag="bank")
                 middle = turn_banks.tile([P, ROWS], F32, name="middle", tag="bank")
-                for bank, i, place in ((middle, 1, 3 * P), (middle, 2, 0), (lower, 3, 0)):
+                mirrored = ((lower, 3, 0), (middle, 1, 3 * P), (middle, 2, 0))
+                for bank, i, place in mirrored:
                     for j in range(i):
                         nc.tensor.transpose(bank[:, place + j * P : place + (j + 1) * P], neg_logits[:, j, i * P : (i + 1) * P], identity[:])
+                for bank, i, place in mirrored:
                     nc.scalar.copy(out=neg_logits[:, i, : i * P], in_=bank[:, place : place + i * P])
             if s > 0:
                 multiply_load(steps[s - 1][0], banks, steps[s - 1][1])

@@ -31,6 +31,8 @@ TEMPERATURE = 0.07
 MASKED = -1.0e30
 POS_A, POS, NEG = 0, 1, 2
 WARM_MATMULS = 5
+VSTEPS = 0
+QSTEPS = 4
 FILLED_STEPS = 2
 
 FLOPS = 2 * 2 * ROWS * ROWS * FEATURES
@@ -109,7 +111,7 @@ def tile_crossgenderinfonceloss_pa_k_kernel(tc, anchor, pos, out):
         def new_grouped():
             return grouped_pool.tile([P, COLUMNS, PACK], BF16, align_bytes=64, name="grouped")
 
-        def transpose_load(n, runs, grouped, chosen):
+        def transpose_load(n, runs, grouped, chosen, shared):
             tiles, passes = shape_of(n)
             grouped_words = grouped[:].bitcast(F32)
             for k in range(BANKS):
@@ -120,16 +122,17 @@ def tile_crossgenderinfonceloss_pa_k_kernel(tc, anchor, pos, out):
                 for u in range(2):
                     for j in range(BANK_TILES):
                         nc.tensor.transpose(bank[:, u, j * P : (j + 1) * P], runs[:, (first + j) * passes + g, u, :], identity[:])
-                nc.scalar.copy(out=grouped_words[:, k * HALF : (k + 1) * HALF], in_=bank[:].rearrange("q u r -> q r u"))
+                copy_out = nc.vector.tensor_copy if shared and k % 2 == 1 else nc.scalar.copy
+                copy_out(out=grouped_words[:, k * HALF : (k + 1) * HALF], in_=bank[:].rearrange("q u r -> q r u"))
 
-        def quantise_load(n, grouped, chosen):
+        def quantise_load(n, grouped, chosen, width):
             tiles, passes = shape_of(n)
-            for first in range(chosen[0] * tiles * P, (chosen[-1] + 1) * tiles * P, ROWS):
-                columns = slice(n * COLUMNS + first, n * COLUMNS + first + ROWS)
+            for first in range(chosen[0] * tiles * P, (chosen[-1] + 1) * tiles * P, width):
+                columns = slice(n * COLUMNS + first, n * COLUMNS + first + width)
                 nc.vector.quantize_mx(
                     out=codes[:, columns].bitcast(FP8X4),
                     scales=scales[:, columns],
-                    in_=grouped[:, first : first + ROWS].rearrange("q c t -> q (c t)"),
+                    in_=grouped[:, first : first + width].rearrange("q c t -> q (c t)"),
                 )
 
         def new_sums():
@@ -234,7 +237,7 @@ def tile_crossgenderinfonceloss_pa_k_kernel(tc, anchor, pos, out):
                     raws[n + LOADS_AHEAD] = start_load(n + LOADS_AHEAD)
             if s + 1 < len(steps):
                 sort_step(s + 1)
-            transpose_load(n, runs[n], groups[n], chosen)
+            transpose_load(n, runs[n], groups[n], chosen, s < VSTEPS)
             if s < FILLED_STEPS:
                 warm_up()
             if n == LOADS + 2:
@@ -248,7 +251,7 @@ def tile_crossgenderinfonceloss_pa_k_kernel(tc, anchor, pos, out):
                     nc.scalar.copy(out=neg_logits[:, i, : i * P], in_=bank[:, place : place + i * P])
             if s > 0:
                 multiply_load(steps[s - 1][0], banks, steps[s - 1][1])
-            quantise_load(n, groups[n], chosen)
+            quantise_load(n, groups[n], chosen, HALF if s < QSTEPS else ROWS)
             if n == LOADS:
                 multiply_middle(banks[3])
                 for i in (0, 2, 3, 1):

from contextlib import ExitStack

import concourse.masks as masks
import concourse.mybir as mybir

F32 = mybir.dt.float32
BF16 = mybir.dt.bfloat16
U32 = mybir.dt.uint32
U8 = mybir.dt.uint8
FP8X4 = mybir.dt.float8_e4m3fn_x4
ACT = mybir.ActivationFunctionType
ALU = mybir.AluOpType

P = 128
PACK = 4
K_PASS = P * PACK
ROWS = 512
ROW_TILES = ROWS // P
HALF = ROWS // 2
FEATURES = 8192
PASSES = FEATURES // K_PASS
BANKS = 4
BANK_TILES = 2
COLUMNS = BANKS * HALF
LOADS = PASSES * ROWS // COLUMNS
HALF_LOADS = LOADS // 2
ALL_LOADS = 2 * LOADS
LOADS_AHEAD = 6
FINE_LOADS = 2
TEMPERATURE = 0.07
MASKED = -1.0e30
POS_A, POS, NEG = 0, 1, 2
WARM_MATMULS = 5
VSTEPS = 0
QSTEPS = 4
FILLED_STEPS = 2

FLOPS = 2 * 2 * ROWS * ROWS * FEATURES


def tile_crossgenderinfonceloss_pa_k_kernel(tc, anchor, pos, out):
    nc = tc.nc
    with ExitStack() as ctx:
        const = ctx.enter_context(tc.tile_pool(name="const", bufs=1))
        keep = ctx.enter_context(tc.tile_pool(name="keep", bufs=1))
        raw_pool = ctx.enter_context(tc.tile_pool(name="raw", bufs=LOADS_AHEAD + 1))
        runs_pool = ctx.enter_context(tc.tile_pool(name="runs", bufs=3))
        grouped_pool = ctx.enter_context(tc.tile_pool(name="grouped", bufs=3))
        sum_banks = ctx.enter_context(tc.psum_pool(name="sum_banks", bufs=1))
        turn_banks = ctx.enter_context(tc.psum_pool(name="turn_banks", bufs=BANKS))
        ctx.enter_context(tc.manual_schedule())

        sources = [x.rearrange("(i p) k -> p i k", p=P) for x in (anchor, pos)]

        codes = keep.tile([P, ALL_LOADS * COLUMNS], U32, align_bytes=64)
        scales = keep.tile([P, ALL_LOADS * COLUMNS], U8, align_bytes=64)

        neg_logits = keep.tile([P, ROW_TILES, ROWS], F32)
        negated = keep.tile([P, 2, ROW_TILES, ROWS], F32)
        shifts = keep.tile([P, 3, ROW_TILES], F32)
        sums = keep.tile([P, 3, ROW_TILES], F32)

        def shape_of(n):
            tiles = ROW_TILES if n < LOADS else BANK_TILES
            return tiles, BANKS * BANK_TILES // tiles

        def pieces_of(n):
            tiles, passes = shape_of(n)
            halves = [(0, 0, BANK_TILES), (0, BANK_TILES, BANK_TILES)] if n == 0 else [(0, 0, tiles)]
            return halves + [(g, 0, tiles) for g in range(1, passes)]

        def start_load(n):
            tiles, passes = shape_of(n)
            features = passes * K_PASS
            raw = raw_pool.tile([P, tiles, features], BF16)
            if n < FINE_LOADS:
                for g, t, width in pieces_of(n):
                    nc.sync.dma_start(
                        out=raw[:, t : t + width, g * K_PASS : (g + 1) * K_PASS],
                        in_=sources[0][:, t : t + width, n * features + g * K_PASS : n * features + (g + 1) * K_PASS],
                    )
            elif n < LOADS:
                nc.sync.dma_start(out=raw[:], in_=sources[0][:, :, n * features : (n + 1) * features])
            else:
                half, part = divmod(n - LOADS, HALF_LOADS)
                nc.sync.dma_start(
                    out=raw[:],
                    in_=sources[1][:, half * BANK_TILES : (half + 1) * BANK_TILES, part * features : (part + 1) * features],
                )
            return raw

        def new_runs():
            return runs_pool.tile([P, BANKS * BANK_TILES, 2, P], F32, name="runs")

        def sort_words(n, raw, runs, chosen):
            tiles, passes = shape_of(n)
            raw_words = raw[:].rearrange("p t k -> p (t k)").bitcast(F32)
            if n < FINE_LOADS:
                source = raw_words.rearrange("p (t g b u q) -> p t g u b q", t=tiles, g=passes, u=2, q=8)
                target = runs[:].rearrange("p (t g) u (b q) -> p t g u b q", t=tiles, q=8)
                for g, t, width in pieces_of(n):
                    if g in chosen:
                        for u in range(2):
                            nc.vector.tensor_copy(out=target[:, t : t + width, g, u], in_=source[:, t : t + width, g, u])
            else:
                source = raw_words.rearrange("p (m b u q) -> p m u b q", m=tiles * passes, u=2, q=8)
                target = runs[:].rearrange("p m u (b q) -> p m u b q", q=8)
                for u in range(2):
                    nc.vector.tensor_copy(out=target[:, :, u], in_=source[:, :, u])

        def new_grouped():
            return grouped_pool.tile([P, COLUMNS, PACK], BF16, align_bytes=64, name="grouped")

        def transpose_load(n, runs, grouped, chosen, shared):
            tiles, passes = shape_of(n)
            grouped_words = grouped[:].bitcast(F32)
            for k in range(BANKS):
                g, first = divmod(k * BANK_TILES, tiles)
                if g not in chosen:
                    continue
                bank = turn_banks.tile([P, 2, HALF], F32)
                for u in range(2):
                    for j in range(BANK_TILES):
                        nc.tensor.transpose(bank[:, u, j * P : (j + 1) * P], runs[:, (first + j) * passes + g, u, :], identity[:])
                copy_out = nc.vector.tensor_copy if shared and k % 2 == 1 else nc.scalar.copy
                copy_out(out=grouped_words[:, k * HALF : (k + 1) * HALF], in_=bank[:].rearrange("q u r -> q r u"))

        def quantise_load(n, grouped, chosen, width):
            tiles, passes = shape_of(n)
            for first in range(chosen[0] * tiles * P, (chosen[-1] + 1) * tiles * P, width):
                columns = slice(n * COLUMNS + first, n * COLUMNS + first + width)
                nc.vector.quantize_mx(
                    out=codes[:, columns].bitcast(FP8X4),
                    scales=scales[:, columns],
                    in_=grouped[:, first : first + width].rearrange("q c t -> q (c t)"),
                )

        def new_sums():
            return [sum_banks.tile([P, ROWS], F32, name="sum%d" % i, tag="sum%d" % i) for i in range(ROW_TILES)]

        LEFT = [0, 2 * P, 2 * P, 3 * P]

        def multiply_load(n, banks, chosen):
            tiles, passes = shape_of(n)
            rows = tiles * P
            for i in range(ROW_TILES):
                left = LEFT[i] if n < LOADS else 0
                for g in chosen:
                    c = (n if n < LOADS else (n - LOADS) % HALF_LOADS) * passes + g
                    stationary = slice(c * ROWS + i * P, c * ROWS + (i + 1) * P)
                    first = n * COLUMNS + g * rows
                    moving = slice(first + left, first + rows)
                    nc.tensor.matmul_mx(
                        out=banks[i][:, left:rows],
                        lhsT=codes[:, stationary].bitcast(FP8X4),
                        lhsT_scale=scales[:, stationary],
                        rhs=codes[:, moving].bitcast(FP8X4),
                        rhs_scale=scales[:, moving],
                        start=(c == 0),
                        stop=(c == PASSES - 1),
                    )

        def multiply_middle(bank):
            for c in range(PASSES):
                block = slice(c * ROWS + P, c * ROWS + 2 * P)
                nc.tensor.matmul_mx(
                    out=bank[:, :P],
                    lhsT=codes[:, block].bitcast(FP8X4),
                    lhsT_scale=scales[:, block],
                    rhs=codes[:, block].bitcast(FP8X4),
                    rhs_scale=scales[:, block],
                    start=(c == 0),
                    stop=(c == PASSES - 1),
                )

        def negate(which, first, i, logits, width, slot, start=None):
            nc.vector.tensor_scalar(
                out=negated[:, which, i, first : first + width],
                in0=logits,
                scalar1=-1.0 / TEMPERATURE,
                scalar2=start,
                op0=ALU.mult,
                op1=ALU.min,
                accum_out=shifts[:, slot, i : i + 1],
            )

        def exponentials(which, first, i, width, slot):
            nc.scalar.activation(
                out=negated[:, which, i, first : first + width],
                in_=negated[:, which, i, first : first + width],
                func=ACT.Exp,
                bias=shifts[:, slot, i : i + 1],
                scale=-1.0,
                accum_out=sums[:, slot, i : i + 1],
            )

        raws = {}
        for n in range(LOADS_AHEAD):
            raws[n] = start_load(n)

        identity = const.tile([P, P], F32)
        masks.make_identity(nc, identity[:])
        masked_diagonal = const.tile([P, P], F32)
        nc.vector.tensor_scalar_mul(out=masked_diagonal[:], in0=identity[:], scalar1=MASKED)
        final = keep.tile([P, 2, P], F32)
        nc.vector.memset(final[:], 0.0)
        warm = const.tile([P, 1], F32)
        nc.vector.memset(warm[:], 0.0)
        nc.scalar.activation(out=warm[:], in_=warm[:], func=ACT.Exp)
        idle = const.tile([P, ROWS], BF16)
        nc.vector.memset(idle[:], 0.0)
        banks = new_sums()

        def warm_up():
            nc.tensor.matmul(banks[3][:], lhsT=idle[:, :P], rhs=idle[:], start=True, stop=True)

        for k in range(WARM_MATMULS):
            warm_up()

        steps = [(n, [g]) for n in range(FINE_LOADS) for g in range(shape_of(n)[1])]
        steps += [(n, list(range(shape_of(n)[1]))) for n in range(FINE_LOADS, ALL_LOADS)]
        runs = {}
        groups = {}

        def sort_step(s):
            n, chosen = steps[s]
            if n not in runs:
                runs[n] = new_runs()
            sort_words(n, raws[n], runs[n], chosen)

        sort_step(0)
        for s in range(len(steps)):
            n, chosen = steps[s]
            if chosen[0] == 0:
                groups[n] = new_grouped()
                if n + LOADS_AHEAD < ALL_LOADS:
                    raws[n + LOADS_AHEAD] = start_load(n + LOADS_AHEAD)
            if s + 1 < len(steps):
                sort_step(s + 1)
            transpose_load(n, runs[n], groups[n], chosen, s < VSTEPS)
            if s < FILLED_STEPS:
                warm_up()
            if n == LOADS + 2:
                lower = turn_banks.tile([P, ROWS], F32, name="lower", tag="bank")
                middle = turn_banks.tile([P, ROWS], F32, name="middle", tag="bank")
                mirrored = ((lower, 3, 0), (middle, 1, 3 * P), (middle, 2, 0))
                for bank, i, place in mirrored:
                    for j in range(i):
                        nc.tensor.transpose(bank[:, place + j * P : place + (j + 1) * P], neg_logits[:, j, i * P : (i + 1) * P], identity[:])
                for bank, i, place in mirrored:
                    nc.scalar.copy(out=neg_logits[:, i, : i * P], in_=bank[:, place : place + i * P])
            if s > 0:
                multiply_load(steps[s - 1][0], banks, steps[s - 1][1])
            quantise_load(n, groups[n], chosen, HALF if s < QSTEPS else ROWS)
            if n == LOADS:
                multiply_middle(banks[3])
                for i in (0, 2, 3, 1):
                    block = slice(i * P, (i + 1) * P)
                    source = banks[3][:, :P] if i == 1 else banks[i][:, block]
                    nc.vector.tensor_add(out=neg_logits[:, i, block], in0=source, in1=masked_diagonal[:])
                nc.scalar.copy(out=neg_logits[:, 0, P:], in_=banks[0][:, P:])
                nc.scalar.copy(out=neg_logits[:, 1, HALF:], in_=banks[1][:, HALF:])
                nc.scalar.copy(out=neg_logits[:, 2, 3 * P :], in_=banks[2][:, 3 * P :])
                banks = new_sums()
            i = n - (LOADS + 2)
            if i in (0, 1):
                negate(1, 0, i, neg_logits[:, i, :], ROWS, NEG)
            if i in (3, 4):
                negate(1, 0, i - 1, neg_logits[:, i - 1, :], ROWS, NEG)
            if i in (1, 2):
                exponentials(1, 0, i - 1, ROWS, NEG)
            if i in (4, 5):
                exponentials(1, 0, i - 2, ROWS, NEG)
            if n == LOADS + HALF_LOADS:
                for i in range(ROW_TILES):
                    negate(0, 0, i, banks[i][:, :HALF], HALF, POS_A)
                banks = new_sums()
            if n in (LOADS + HALF_LOADS + 1, LOADS + HALF_LOADS + 3):
                for i in (n - LOADS - HALF_LOADS - 1, n - LOADS - HALF_LOADS):
                    exponentials(0, 0, i, HALF, POS_A)
        multiply_load(steps[-1][0], banks, steps[-1][1])
        for i in range(ROW_TILES):
            negate(0, HALF, i, banks[i][:, :HALF], HALF, POS, shifts[:, POS_A, i : i + 1])
            exponentials(0, HALF, i, HALF, POS)

        gaps = keep.tile([P, 3, ROW_TILES], F32)
        weights = keep.tile([P, 3, ROW_TILES], F32)
        weighted = keep.tile([P, ROW_TILES], F32)
        minus_top = keep.tile([P, ROW_TILES], F32)
        total_pos = keep.tile([P, ROW_TILES], F32)
        inverse = keep.tile([P, ROW_TILES], F32)
        nc.vector.tensor_tensor(out=minus_top[:], in0=shifts[:, POS, :], in1=shifts[:, NEG, :], op=ALU.min)
        nc.vector.tensor_sub(out=gaps[:, POS_A, :], in0=shifts[:, POS, :], in1=shifts[:, POS_A, :])
        nc.vector.tensor_sub(
            out=gaps[:, POS:, :],
            in0=minus_top[:].unsqueeze(1).to_broadcast([P, 2, ROW_TILES]),
            in1=shifts[:, POS:, :],
        )
        nc.scalar.activation(out=weights[:], in_=gaps[:], func=ACT.Exp)
        nc.scalar.activation(out=warm[:], in_=warm[:], func=ACT.Ln)
        nc.vector.tensor_copy(out=final[:, 1, :ROW_TILES], in_=gaps[:, POS, :])
        nc.vector.tensor_mul(out=weighted[:], in0=sums[:, NEG, :], in1=weights[:, NEG, :])
        for i in range(ROW_TILES):
            one = slice(i, i + 1)
            nc.vector.scalar_tensor_tensor(
                out=total_pos[:, one],
                in0=sums[:, POS_A, one],
                scalar=weights[:, POS_A, one],
                in1=sums[:, POS, one],
                op0=ALU.mult,
                op1=ALU.add,
            )
        nc.vector.reciprocal(out=inverse[:], in_=total_pos[:])
        for i in range(ROW_TILES):
            one = slice(i, i + 1)
            nc.vector.scalar_tensor_tensor(
                out=final[:, 0, one],
                in0=inverse[:, one],
                scalar=weighted[:, one],
                in1=weights[:, POS, one],
                op0=ALU.mult,
                op1=ALU.add,
            )
        turned = turn_banks.tile([P, 2, P], F32, name="turned", tag="bank")
        nc.tensor.transpose(turned[:, 1, :], final[:, 1, :], identity[:])
        nc.tensor.transpose(turned[:, 0, :], final[:, 0, :], identity[:])
        logs = keep.tile([P, P], F32)
        results = keep.tile([P, P], F32)
        nc.scalar.activation(out=logs[:ROW_TILES, :], in_=turned[:ROW_TILES, 0, :], func=ACT.Ln)
        nc.vector.tensor_sub(out=results[:ROW_TILES, :], in0=turned[:ROW_TILES, 1, :], in1=logs[:ROW_TILES, :])
        nc.sync.dma_start(out=out.rearrange("(i p) -> i p", p=P), in_=results[:ROW_TILES, :])
